import numpy as np
import ml_dtypes


BF16 = ml_dtypes.bfloat16


def bf(x):
    return np.asarray(x, np.float32).astype(BF16)


def f64(x):
    return np.asarray(x).astype(np.float64)


E2M1 = np.array([0.0, 0.5, 1.0, 1.5, 2.0, 3.0, 4.0, 6.0, -0.0, -0.5, -1.0, -1.5, -2.0, -3.0, -4.0, -6.0])


def pack_weight(w, fmt):
    k, n = w.shape
    w = f64(bf(w)).reshape(k // 32, 32, n)
    amax = np.abs(w).max(1)
    if fmt == "e4m3":
        byte = np.frexp(amax)[1] - 1 + 127 - 7
    else:
        mant, ex = np.frexp(amax / 6.0)
        byte = np.where(mant > 0.5, ex, ex - 1) + 127
    byte = np.clip(np.where(amax > 0, byte, 1), 1, 254)
    scaled = (w * np.exp2(127.0 - byte)[:, None, :]).reshape(k, n).astype(np.float32)
    by_word = np.ascontiguousarray(scaled.reshape(k // 512, 128, 4, n).transpose(0, 1, 3, 2))
    if fmt == "e4m3":
        words = by_word.astype(ml_dtypes.float8_e4m3fn).view(np.uint8)
    else:
        c = by_word.astype(ml_dtypes.float4_e2m1fn).view(np.uint8) & 0xF
        words = c[..., 0::2] | (c[..., 1::2] << 4)
    return np.ascontiguousarray(words), np.ascontiguousarray(byte.astype(np.uint8).reshape(k // 512, 16, n))


def unpack_weight(words, scales, fmt):
    g, p, n, _ = words.shape
    if fmt == "e4m3":
        vals = np.ascontiguousarray(words).view(ml_dtypes.float8_e4m3fn).astype(np.float64)
    else:
        nib = np.empty((g, p, n, 4), np.uint8)
        nib[..., 0::2] = words & 0xF
        nib[..., 1::2] = words >> 4
        vals = E2M1[nib]
    vals = vals * np.repeat(np.exp2(scales.astype(np.float64) - 127.0), 8, axis=1)[..., None]
    return vals.transpose(0, 1, 3, 2).reshape(g * 512, n)

def pack4(w):
    words, scales = pack_weight(w, "e2m1")
    return words.reshape(words.shape[0], 128, -1), scales


def unpack4(words, scales):
    return unpack_weight(words.reshape(words.shape[0], 128, -1, 2), scales, "e2m1")


def kspread(k):
    return np.exp2(np.repeat(np.random.randint(-6, 7, k // 32), 32).astype(np.float64))


B, T, E, H, FF = 4, 512, 1024, 8, 8192
EPS = 1e-5


def layernorm(r, g):
    mu = r.mean(-1, keepdims=True)
    var = ((r - mu) ** 2).mean(-1, keepdims=True)
    return (r - mu) / np.sqrt(var + EPS) * g


def setup_inputs():
    t = kspread(FF)
    z = np.random.standard_normal((B, T, FF))
    y_act = z * z / (1.0 + np.exp(-z)) * t
    y_act_words, y_act_scales = pack4(y_act.reshape(B * T, FF).T)
    h = bf(np.random.standard_normal((B, T, E)))
    W2_words, W2_scales = pack4(np.random.standard_normal((FF, E)) / np.sqrt(FF) / t[:, None])
    return {
        "y_act_words": y_act_words,
        "y_act_scales": y_act_scales,
        "h": h,
        "W2_words": W2_words,
        "W2_scales": W2_scales,
        "b2": bf(np.random.standard_normal(E) * 0.1),
        "g2": bf(1.0 + np.random.standard_normal(E) * 0.1),
    }


def reference(y_act_words, y_act_scales, h, W2_words, W2_scales, b2, g2):
    ya = unpack4(y_act_words, y_act_scales).T.reshape(B, T, FF)
    ff = (ya @ unpack4(W2_words, W2_scales)) + f64(b2)
    return layernorm(ff + f64(h), f64(g2))

from contextlib import ExitStack

import concourse.mybir as mybir

TOKENS, E, FF = 2048, 1024, 8192
EPS = 1e-5

F32 = mybir.dt.float32
BF16 = mybir.dt.bfloat16
U8 = mybir.dt.uint8
I32 = mybir.dt.int32
FP4X4 = mybir.dt.float4_e2m1fn_x4
ACT = mybir.ActivationFunctionType
ALU = mybir.AluOpType

P = 128
PASSES = FF // 512
BLOCK = 512
BLOCKS = TOKENS // BLOCK
TILES = TOKENS // P
TPB = BLOCK // P
BANK = 512
HALVES = E // BANK

FLOPS = 2 * TOKENS * E * FF

CODE_RUNS = ((0, 1), (1, 2), (2, 4), (4, 7), (7, 11), (11, 16))
SCALE_RUNS = ((0, 2), (2, 7), (7, 16))
SPLIT_PASS = 8
WARM = 6
TAIL_CHUNKS = ((0, 320), (320, 640), (640, 896), (896, 1024))


def locate(runs, g):
    for index, (lo, hi) in enumerate(runs):
        if lo <= g < hi:
            return index, g - lo
    raise ValueError("pass outside the runs")


def tile_transformerblock_pb_t_kernel(tc, y_words, y_scales, h, w_words, w_scales, b2, g2, out):
    nc = tc.nc
    h_rows = h.flatten_outer_dims()
    out_rows = out.flatten_outer_dims()

    with ExitStack() as ctx:
        keep = ctx.enter_context(tc.tile_pool(name="keep", bufs=1))
        work = ctx.enter_context(tc.tile_pool(name="work", bufs=2))
        psum = ctx.enter_context(tc.psum_pool(name="psum", bufs=1))
        ctx.enter_context(tc.manual_schedule())

        def kept(name, shape, dtype):
            return keep.tile(shape, dtype, name=name, tag=name, align_bytes=256)

        w_codes = [kept("w_codes%d" % i, [P, hi - lo, 2 * E], U8) for i, (lo, hi) in enumerate(CODE_RUNS)]
        w_planes = [kept("w_planes%d" % i, [P, hi - lo, E], U8) for i, (lo, hi) in enumerate(SCALE_RUNS)]
        y0_codes = [kept("y0_codes%d" % i, [P, hi - lo, 2 * BLOCK], U8) for i, (lo, hi) in enumerate(CODE_RUNS)]
        y0_planes = [kept("y0_planes%d" % i, [P, hi - lo, BLOCK], U8) for i, (lo, hi) in enumerate(SCALE_RUNS)]
        HALF = PASSES // 2
        yb_codes = {
            (b, u): kept("y%d_codes%d" % (b, u), [P, HALF, 2 * BLOCK], U8) for b in range(1, BLOCKS) for u in range(2)
        }
        yb_planes = {b: kept("y%d_planes" % b, [P, PASSES, BLOCK], U8) for b in range(1, BLOCKS)}
        h_sb = [kept("h%d" % b, [P, TPB, E], BF16) for b in range(BLOCKS)]
        b2_sb = kept("b2_sb", [P, E], BF16)
        g2_sb = kept("g2_sb", [P, E], BF16)
        zeros = kept("zeros", [P, BANK], BF16)
        preload = kept("preload", [P, 1], F32)

        def load_codes(dst, src, lo, hi, c0, c1):
            nc.sync.dma_start(
                out=dst[:].bitcast(I32), in_=src[lo:hi, :, c0:c1].rearrange("g p n -> p g n").bitcast(I32)
            )

        def load_scales(dst, src, lo, hi, c0, c1):
            for q in range(4):
                nc.sync.dma_start(
                    out=dst[32 * q : 32 * q + 4, :, :].bitcast(I32),
                    in_=src[lo:hi, 4 * q : 4 * q + 4, c0:c1].rearrange("g r n -> r g n").bitcast(I32),
                )

        def zero_plane(plane):
            nc.vector.memset(plane[:].bitcast(I32), 0)

        nc.vector.memset(zeros[:], 0.0)
        for i in range(len(SCALE_RUNS)):
            zero_plane(y0_planes[i])
            zero_plane(w_planes[i])
            if i == 0:
                nc.vector.memset(preload[:], 1.0)
        for b in range(1, BLOCKS):
            zero_plane(yb_planes[b])
        nc.scalar.activation(out=preload[:], in_=preload[:], func=ACT.Abs_reciprocal_sqrt)

        def codes_run(i):
            lo, hi = CODE_RUNS[i]
            load_codes(y0_codes[i], y_words, lo, hi, 0, 2 * BLOCK)
            load_codes(w_codes[i], w_words, lo, hi, 0, 2 * E)

        def scales_run(i):
            lo, hi = SCALE_RUNS[i]
            load_scales(y0_planes[i], y_scales, lo, hi, 0, BLOCK)
            load_scales(w_planes[i], w_scales, lo, hi, 0, E)

        codes_run(0)
        scales_run(0)
        codes_run(1)
        codes_run(2)
        scales_run(1)
        codes_run(3)
        scales_run(2)
        codes_run(4)
        codes_run(5)

        def load_h(b):
            nc.sync.dma_start(
                out=h_sb[b][:], in_=h_rows[BLOCK * b : BLOCK * (b + 1), :].rearrange("(i p) e -> p i e", p=P)
            )

        load_h(0)
        nc.sync.dma_start(out=b2_sb[:], in_=b2.partition_broadcast(P))
        nc.sync.dma_start(out=g2_sb[:], in_=g2.partition_broadcast(P))
        for b in range(1, BLOCKS):
            load_scales(yb_planes[b], y_scales, 0, PASSES, BLOCK * b, BLOCK * (b + 1))
            for u in range(2):
                load_codes(
                    yb_codes[b, u], y_words, HALF * u, HALF * (u + 1), 2 * BLOCK * b, 2 * BLOCK * (b + 1)
                )
            load_h(b)

        def bank(k, cols=BANK):
            return psum.tile([P, cols], F32, name="bank%d" % k, tag="bank%d" % k)

        def one_pass(acc, t, c0, cols, g):
            b, i = divmod(t, TPB)
            cr, cj = locate(CODE_RUNS, g)
            sr, sj = locate(SCALE_RUNS, g)
            if b == 0:
                codes, planes = y0_codes[cr][:, cj, :], y0_planes[sr][:, sj, :]
            else:
                codes, planes = yb_codes[b, g // HALF][:, g % HALF, :], yb_planes[b][:, g, :]
            nc.tensor.matmul_mx(
                out=acc[:, 0:cols],
                lhsT=codes[:, 2 * P * i : 2 * P * (i + 1)].bitcast(FP4X4),
                lhsT_scale=planes[:, P * i : P * (i + 1)],
                rhs=w_codes[cr][:, cj, 2 * c0 : 2 * (c0 + cols)].bitcast(FP4X4),
                rhs_scale=w_planes[sr][:, sj, c0 : c0 + cols],
                start=(g == 0),
                stop=(g == PASSES - 1),
            )

        hb = {}
        r = {}
        stats = {}

        def residual(t):
            b, i = divmod(t, TPB)
            hb[t] = work.tile([P, E], F32, name="hb", tag="hb", bufs=5)
            nc.vector.tensor_tensor(out=hb[t][:], in0=h_sb[b][:, i, :], in1=b2_sb[:], op=ALU.add)

        def add_and_stats(t, acc, c0, cols, slot):
            cs = slice(c0, c0 + cols)
            nc.vector.tensor_tensor(out=r[t][:, cs], in0=acc[:, 0:cols], in1=hb[t][:, cs], op=ALU.add)
            nc.vector.bn_stats(out=stats[t][:, slot, :], in_=r[t][:, cs])

        def normalise(t, chunks):
            mv = work.tile([P, 2], F32, name="mv", tag="mv")
            rstd = work.tile([P, 1], F32, name="rstd", tag="rstd")
            scaled = work.tile([P, E], F32, name="scaled", tag="scaled")
            res = work.tile([P, E], F32, name="res", tag="res", bufs=3)
            nc.vector.bn_aggr(out=mv[:], in_=stats[t][:].rearrange("p s k -> p (s k)"))
            nc.scalar.activation(out=rstd[:], in_=mv[:, 1:2], func=ACT.Abs_reciprocal_sqrt, bias=EPS, scale=1.0)
            for c0, c1 in chunks:
                cs = slice(c0, c1)
                nc.vector.scalar_tensor_tensor(
                    out=scaled[:, cs],
                    in0=r[t][:, cs],
                    scalar=mv[:, 0:1],
                    in1=g2_sb[:, cs],
                    op0=ALU.subtract,
                    op1=ALU.mult,
                )
                nc.scalar.activation(out=res[:, cs], in_=scaled[:, cs], func=ACT.Copy, scale=rstd[:])
                nc.sync.dma_start(out=out_rows[P * t : P * (t + 1), cs], in_=res[:, cs])

        def open_rows(t, slots):
            r[t] = work.tile([P, E], F32, name="r", tag="r")
            stats[t] = work.tile([P, slots, 6], F32, name="stats%d" % slots, tag="stats%d" % slots)

        warm = bank(7)
        for i in range(WARM):
            nc.tensor.matmul(out=warm[:], lhsT=zeros[:, 0:P], rhs=zeros[:], start=True, stop=True)

        for t in range(TPB):
            residual(t)

        accs = {}
        for g in range(SPLIT_PASS):
            for t in range(TPB):
                for n in range(HALVES):
                    if g == 0:
                        accs[t, n] = bank(HALVES * t + n)
                    one_pass(accs[t, n], t, BANK * n, BANK, g)

        for t in range(TILES):
            if t < TILES - 1:
                pieces = [(BANK * n, BANK) for n in range(HALVES)]
            else:
                pieces = [(0, 512), (512, 256), (768, 256)]
            open_rows(t, len(pieces))
            for n, (c0, cols) in enumerate(pieces):
                if t < TPB:
                    acc = accs[t, n]
                    first = SPLIT_PASS
                else:
                    acc = bank((HALVES * t + n) % 8, cols)
                    first = 0
                for g in range(first, PASSES):
                    one_pass(acc, t, c0, cols, g)
                add_and_stats(t, acc, c0, cols, n)
            normalise(t, ((0, E),) if t < TILES - 1 else TAIL_CHUNKS)
            if t + TPB < TILES:
                residual(t + TPB)
